import numpy as np
import ml_dtypes


def mxq(x, axis, fmt="e4m3"):
    dtype, down = {"e4m3": (ml_dtypes.float8_e4m3fn, 7), "e5m2": (ml_dtypes.float8_e5m2, 14)}[fmt]
    v = np.moveaxis(np.asarray(x, np.float32).astype(ml_dtypes.bfloat16).astype(np.float64), axis, -1)
    blocks = v.reshape(v.shape[:-1] + (-1, 32))
    amax = np.abs(blocks).max(-1, keepdims=True)
    byte = np.maximum(np.where(amax > 0, np.frexp(amax)[1] - 1 + 127, 0) - down, 1)
    scale = np.exp2(byte - 127.0)
    codes = (blocks / scale).astype(np.float32).astype(dtype).astype(np.float64)
    return np.moveaxis((codes * scale).reshape(v.shape), -1, axis)


BF16 = ml_dtypes.bfloat16


def bf(x):
    return np.asarray(x, np.float32).astype(BF16)


def f64(x):
    return np.asarray(x).astype(np.float64)


N, D, K = 4096, 512, 512
S = 5.0


def setup_inputs():
    m = np.random.standard_normal(D) / np.sqrt(D)
    return {"data": bf(m + np.random.standard_normal((N, D)) * 0.4 / np.sqrt(D)),
            "centers": bf(m + np.random.standard_normal((K, D)) * 0.4 / np.sqrt(D))}


def reference(data, centers):
    data, centers = f64(data), f64(centers)
    x2 = np.sum(data * data, axis=-1, keepdims=True)
    c2 = np.sum(centers * centers, axis=-1)[None, :]
    xc = mxq(data, 1, "e4m3") @ mxq(centers, 1, "e4m3").T
    r2 = x2 + c2 - 2.0 * xc
    rbfs = np.exp(-S * r2)
    ones = np.ones((data.shape[0], 1))
    return np.concatenate([ones, data, rbfs], axis=-1)

@@ -1,0 +1,232 @@
+from contextlib import ExitStack
+
+import concourse.masks as masks
+import concourse.mybir as mybir
+
+FLOPS = 2 * 4096 * 512 * 512
+
+F32 = mybir.dt.float32
+BF16 = mybir.dt.bfloat16
+U32 = mybir.dt.uint32
+U8 = mybir.dt.uint8
+FP8X4 = mybir.dt.float8_e4m3fn_x4
+ACT = mybir.ActivationFunctionType
+ALU = mybir.AluOpType
+
+P = 128
+D = 512
+K = 512
+W = 1 + D + K
+T = 4096 // P
+GR = 4
+NG = T // GR
+CH = 8
+LOADS = (4, 4, 8, 8, 8)
+VROWS = 4
+LEAD = 6
+STORE_CUTS = (2, 4, 6, 8, 12, 16, 20, 24, 28, 30, 32)
+
+
+def tile_dicgaussianrbf_t_kernel(tc, data, centers, out):
+    nc = tc.nc
+    with ExitStack() as ctx:
+        keep = ctx.enter_context(tc.tile_pool(name="keep", bufs=1))
+        work = ctx.enter_context(tc.tile_pool(name="work", bufs=3))
+        tmps = ctx.enter_context(tc.tile_pool(name="tmps", bufs=8))
+        psum = ctx.enter_context(tc.psum_pool(name="psum", bufs=4))
+        ctx.enter_context(tc.manual_schedule())
+
+        data_v = data.rearrange("(p t) d -> p t d", t=T)
+        out_v = out.rearrange("(p t) c -> p (t c)", t=T)
+
+        ident = keep.tile([P, P], F32, name="ident")
+        masks.make_identity(nc, ident[:])
+        warm = keep.tile([P, 1], F32, name="warm")
+        warm2 = keep.tile([P, 1], F32, name="warm2")
+        nc.vector.memset(warm[:], 0.0)
+        nc.scalar.activation(out=warm2[:], in_=warm[:], func=ACT.Exp)
+
+        cen = keep.tile([P, 4, D], BF16, name="cen")
+        nc.sync.dma_start(out=cen[:], in_=centers.rearrange("(j p) d -> p j d", p=P))
+        rows = []
+        t0 = 0
+        for li, n in enumerate(LOADS):
+            dtile = keep.tile([P, n, D], BF16, name="d%d" % li)
+            nc.sync.dma_start(out=dtile[:], in_=data_v[:, t0 : t0 + n, :])
+            for r in range(n):
+                rows.append(dtile[:, r, :])
+            t0 += n
+
+        o_tiles = []
+        o_views = []
+        for c in range(T // CH):
+            ot = keep.tile([P, CH * W], F32, name="o%d" % c)
+            o_tiles.append(ot)
+            o_views.append(ot[:].rearrange("p (t c) -> p t c", c=W))
+
+        def o_row(t):
+            return o_views[t // CH][:, t % CH, :]
+
+        for c in range(T // CH):
+            lo = c * CH
+            nv = min(max(VROWS - lo, 0), CH)
+            if nv > 0:
+                nc.vector.memset(o_views[c][:, 0:nv, 0:1], 1.0)
+            if nv < CH:
+                nc.gpsimd.memset(o_views[c][:, nv:CH, 0:1], 1.0)
+
+        x2 = keep.tile([P, T], F32, name="x2")
+        nb = keep.tile([P, T], F32, name="nb")
+        c2col = keep.tile([P, 4], F32, name="c2col")
+        junk = keep.tile([P, D], BF16, name="junk")
+        rep = keep.tile([P, 4, P], F32, name="rep")
+        c2h = keep.tile([P, K], F32, name="c2h")
+        c_codes = keep.tile([P, K], U32, name="c_codes", align_bytes=64)
+        c_scl = keep.tile([P, K], U8, name="c_scl", align_bytes=64)
+
+        banks = {}
+        grps = {}
+        quant = {}
+        xcs = {}
+        tmp_of = {}
+        st = {"cut": 0, "gk": VROWS, "m": 0}
+
+        def transposes(key, srcs):
+            pair = []
+            for b in range(2):
+                tp = psum.tile([P, 512], F32, tag="tp", name="tp")
+                for a in range(2):
+                    src = srcs[2 * b + a].bitcast(F32)
+                    for u in range(2):
+                        s = (2 * a + u) * P
+                        nc.tensor.transpose(tp[:, s : s + P], src[:, u * P : (u + 1) * P], ident[:])
+                pair.append(tp)
+            banks[key] = pair
+
+        def t_data(g):
+            transposes(g, rows[g * GR : (g + 1) * GR])
+
+        def copy_out(key, b):
+            if b == 0:
+                grp = work.tile([P, 4 * 512], BF16, tag="grp", name="grp", align_bytes=64)
+                grps[key] = grp
+            g32 = grps[key][:].bitcast(F32)
+            nc.vector.tensor_copy(
+                out=g32[:, 512 * b : 512 * (b + 1)].rearrange("q (a n u) -> q a n u", a=2, u=2),
+                in_=banks[key][b][:].rearrange("q (a u n) -> q a n u", a=2, u=2),
+            )
+
+        def quantise(key):
+            if key == "c":
+                codes, scl = c_codes, c_scl
+            else:
+                codes = work.tile([P, 512], U32, tag="codes", name="codes", align_bytes=64)
+                scl = work.tile([P, 512], U8, tag="scl", name="scl", align_bytes=64)
+            nc.vector.quantize_mx(out=codes[:].bitcast(FP8X4), scales=scl[:], in_=grps[key][:])
+            quant[key] = (codes, scl)
+
+        def mx(t):
+            codes, scl = quant[t // GR]
+            a = t % GR
+            xc = psum.tile([P, K], F32, tag="xc", name="xc")
+            nc.tensor.matmul_mx(
+                out=xc[:],
+                lhsT=codes[:, a * P : (a + 1) * P].bitcast(FP8X4),
+                lhsT_scale=scl[:, a * P : (a + 1) * P],
+                rhs=c_codes[:].bitcast(FP8X4),
+                rhs_scale=c_scl[:],
+                start=True,
+                stop=True,
+            )
+            xcs[t] = xc
+
+        def sub_c2(t):
+            tmp = tmps.tile([P, K], F32, tag="tmp", name="tmp")
+            nc.vector.tensor_tensor(out=tmp[:], in0=xcs[t][:], in1=c2h[:], op=ALU.subtract)
+            tmp_of[t] = tmp
+
+        def cast_v(t):
+            nc.vector.tensor_copy(out=o_row(t)[:, 1 : 1 + D], in_=rows[t])
+
+        def casts_g(upto):
+            for t in range(st["gk"], min(upto, T - 1) + 1):
+                nc.gpsimd.tensor_scalar(
+                    out=o_row(t)[:, 1 : 1 + D], in0=rows[t], scalar1=1.0, scalar2=0.0,
+                    op0=ALU.mult, op1=ALU.add,
+                )
+            st["gk"] = max(st["gk"], min(upto, T - 1) + 1)
+
+        def square(t):
+            nc.scalar.activation(out=junk[:], in_=rows[t], func=ACT.Square, accum_out=x2[:, t : t + 1])
+            if t % GR == GR - 1:
+                g = t // GR
+                casts_g(t + GR)
+                nc.gpsimd.tensor_scalar(
+                    out=nb[:, g * GR : (g + 1) * GR], in0=x2[:, g * GR : (g + 1) * GR],
+                    scalar1=-5.0, scalar2=0.0, op0=ALU.mult, op1=ALU.add,
+                )
+
+        def store(r0, r1):
+            c = r0 // CH
+            a = ((r0 % CH) * W) // 8 * 8
+            b = CH * W if r1 % CH == 0 else ((r1 % CH) * W) // 8 * 8
+            nc.sync.dma_start(out=out_v[:, c * CH * W + a : c * CH * W + b], in_=o_tiles[c][:, a:b])
+
+        def expo(t):
+            nc.scalar.activation(
+                out=o_row(t)[:, 1 + D : W], in_=tmp_of[t][:], func=ACT.Exp,
+                bias=nb[:, t : t + 1], scale=10.0,
+            )
+            if t + 1 in STORE_CUTS:
+                store(st["cut"], t + 1)
+                st["cut"] = t + 1
+
+        def passes(t_done):
+            for r in range(st["m"], min(t_done + GR, T - 1) + 1):
+                if r // GR in quant:
+                    mx(r)
+                    st["m"] = r + 1
+
+        transposes("c", [cen[:, j, :] for j in range(4)])
+        t_data(0)
+        for j in range(4):
+            nc.scalar.activation(out=junk[:], in_=cen[:, j, :], func=ACT.Square, accum_out=c2col[:, j : j + 1])
+        copy_out("c", 0)
+        copy_out("c", 1)
+        copy_out(0, 0)
+        copy_out(0, 1)
+        t_data(1)
+        quantise("c")
+        nc.vector.tensor_copy(out=rep[:], in_=c2col[:].unsqueeze(2).to_broadcast([P, 4, P]))
+        c2ps = psum.tile([P, K], F32, tag="xc", name="c2ps")
+        for j in range(4):
+            nc.tensor.transpose(c2ps[:, j * P : (j + 1) * P], rep[:, j, :], ident[:])
+        quantise(0)
+        for t in range(min(2, VROWS)):
+            cast_v(t)
+        nc.vector.tensor_scalar(out=c2h[:], in0=c2ps[:], scalar1=0.5, scalar2=None, op0=ALU.mult)
+        passes(-1)
+        t_data(2)
+        for t in range(LEAD):
+            square(t)
+
+        aux = []
+        for g in range(1, NG):
+            aux.extend([("c", g, 0), ("c", g, 1), ("q", g, 0)])
+
+        for t in range(T):
+            sub_c2(t)
+            if t + 2 < VROWS:
+                cast_v(t + 2)
+            expo(t)
+            if t + LEAD < T:
+                square(t + LEAD)
+            if t < len(aux):
+                kind, g, b = aux[t]
+                if kind == "c":
+                    copy_out(g, b)
+                    if b == 1 and g + 2 < NG:
+                        t_data(g + 2)
+                else:
+                    quantise(g)
+            passes(t)

@@ -1,3 +1,4 @@
+import math
 from contextlib import ExitStack
 
 import concourse.masks as masks
@@ -22,8 +23,10 @@ GR = 4
 NG = T // GR
 CH = 8
 LOADS = (4, 4, 8, 8, 8)
-VROWS = 4
-LEAD = 6
+ROOT_HALF = math.sqrt(0.5)
+GRAM_GROUPS = (2, 4, 6)
+SCALAR_COPIES = (1, 2, 3, 4, 5, 6, 7)
+XC_BUFS = 3
 STORE_CUTS = (2, 4, 6, 8, 12, 16, 20, 24, 28, 30, 32)
 
 
@@ -32,7 +35,7 @@ def tile_dicgaussianrbf_t_kernel(tc, data, centers, out):
     with ExitStack() as ctx:
         keep = ctx.enter_context(tc.tile_pool(name="keep", bufs=1))
         work = ctx.enter_context(tc.tile_pool(name="work", bufs=3))
-        tmps = ctx.enter_context(tc.tile_pool(name="tmps", bufs=8))
+        tmps = ctx.enter_context(tc.tile_pool(name="tmps", bufs=6))
         psum = ctx.enter_context(tc.psum_pool(name="psum", bufs=4))
         ctx.enter_context(tc.manual_schedule())
 
@@ -67,19 +70,10 @@ def tile_dicgaussianrbf_t_kernel(tc, data, centers, out):
         def o_row(t):
             return o_views[t // CH][:, t % CH, :]
 
-        for c in range(T // CH):
-            lo = c * CH
-            nv = min(max(VROWS - lo, 0), CH)
-            if nv > 0:
-                nc.vector.memset(o_views[c][:, 0:nv, 0:1], 1.0)
-            if nv < CH:
-                nc.gpsimd.memset(o_views[c][:, nv:CH, 0:1], 1.0)
-
-        x2 = keep.tile([P, T], F32, name="x2")
-        nb = keep.tile([P, T], F32, name="nb")
+        x2h = keep.tile([P, T], F32, name="x2h")
         c2col = keep.tile([P, 4], F32, name="c2col")
         junk = keep.tile([P, D], BF16, name="junk")
-        rep = keep.tile([P, 4, P], F32, name="rep")
+        junk_g = keep.tile([P, P], F32, name="junk_g")
         c2h = keep.tile([P, K], F32, name="c2h")
         c_codes = keep.tile([P, K], U32, name="c_codes", align_bytes=64)
         c_scl = keep.tile([P, K], U8, name="c_scl", align_bytes=64)
@@ -88,8 +82,9 @@ def tile_dicgaussianrbf_t_kernel(tc, data, centers, out):
         grps = {}
         quant = {}
         xcs = {}
+        grams = {}
         tmp_of = {}
-        st = {"cut": 0, "gk": VROWS, "m": 0}
+        st = {"cut": 0, "m": 0, "ready": 0}
 
         def transposes(key, srcs):
             pair = []
@@ -106,29 +101,54 @@ def tile_dicgaussianrbf_t_kernel(tc, data, centers, out):
         def t_data(g):
             transposes(g, rows[g * GR : (g + 1) * GR])
 
-        def copy_out(key, b):
-            if b == 0:
+        def copy_out(key, b, on_scalar=False):
+            if key not in grps:
                 grp = work.tile([P, 4 * 512], BF16, tag="grp", name="grp", align_bytes=64)
                 grps[key] = grp
             g32 = grps[key][:].bitcast(F32)
-            nc.vector.tensor_copy(
-                out=g32[:, 512 * b : 512 * (b + 1)].rearrange("q (a n u) -> q a n u", a=2, u=2),
-                in_=banks[key][b][:].rearrange("q (a u n) -> q a n u", a=2, u=2),
-            )
-
-        def quantise(key):
-            if key == "c":
-                codes, scl = c_codes, c_scl
+            dst = g32[:, 512 * b : 512 * (b + 1)].rearrange("q (a n u) -> q a n u", a=2, u=2)
+            src = banks[key][b][:].rearrange("q (a u n) -> q a n u", a=2, u=2)
+            if on_scalar:
+                nc.scalar.copy(out=dst, in_=src)
             else:
+                nc.vector.tensor_copy(out=dst, in_=src)
+
+        def quantise(key, lo=0, hi=512):
+            if key == "c":
+                quant[key] = (c_codes, c_scl)
+            elif key not in quant:
                 codes = work.tile([P, 512], U32, tag="codes", name="codes", align_bytes=64)
                 scl = work.tile([P, 512], U8, tag="scl", name="scl", align_bytes=64)
-            nc.vector.quantize_mx(out=codes[:].bitcast(FP8X4), scales=scl[:], in_=grps[key][:])
-            quant[key] = (codes, scl)
+                quant[key] = (codes, scl)
+            codes, scl = quant[key]
+            nc.vector.quantize_mx(
+                out=codes[:, lo:hi].bitcast(FP8X4), scales=scl[:, lo:hi], in_=grps[key][:, 4 * lo : 4 * hi]
+            )
+            if key != "c":
+                st["ready"] = key * GR + hi // P
+
+        def gram(g):
+            gm = psum.tile([P, GR, P], F32, tag="gm", name="gm", bufs=1)
+            v = grps[g][:].rearrange("p (r n j) -> p r j n", r=GR, j=4)
+            for r in range(GR):
+                for j in range(4):
+                    nc.tensor.matmul(
+                        out=gm[:, r, :], lhsT=v[:, r, j, :], rhs=v[:, r, j, :],
+                        start=(j == 0), stop=(j == 3),
+                    )
+            grams[g] = gm
+
+        def diag(g, r):
+            t = g * GR + r
+            nc.vector.scalar_tensor_tensor(
+                out=junk_g[:], in0=grams[g][:, r, :], scalar=0.5, in1=ident[:],
+                op0=ALU.mult, op1=ALU.mult, accum_out=x2h[:, t : t + 1],
+            )
 
         def mx(t):
             codes, scl = quant[t // GR]
             a = t % GR
-            xc = psum.tile([P, K], F32, tag="xc", name="xc")
+            xc = psum.tile([P, K], F32, tag="xc", name="xc", bufs=XC_BUFS)
             nc.tensor.matmul_mx(
                 out=xc[:],
                 lhsT=codes[:, a * P : (a + 1) * P].bitcast(FP8X4),
@@ -140,31 +160,18 @@ def tile_dicgaussianrbf_t_kernel(tc, data, centers, out):
             )
             xcs[t] = xc
 
-        def sub_c2(t):
+        def sub(t):
             tmp = tmps.tile([P, K], F32, tag="tmp", name="tmp")
-            nc.vector.tensor_tensor(out=tmp[:], in0=xcs[t][:], in1=c2h[:], op=ALU.subtract)
+            nc.vector.scalar_tensor_tensor(
+                out=tmp[:], in0=xcs[t][:], scalar=x2h[:, t : t + 1], in1=c2h[:],
+                op0=ALU.subtract, op1=ALU.subtract,
+            )
             tmp_of[t] = tmp
 
-        def cast_v(t):
-            nc.vector.tensor_copy(out=o_row(t)[:, 1 : 1 + D], in_=rows[t])
-
-        def casts_g(upto):
-            for t in range(st["gk"], min(upto, T - 1) + 1):
-                nc.gpsimd.tensor_scalar(
-                    out=o_row(t)[:, 1 : 1 + D], in0=rows[t], scalar1=1.0, scalar2=0.0,
-                    op0=ALU.mult, op1=ALU.add,
-                )
-            st["gk"] = max(st["gk"], min(upto, T - 1) + 1)
-
         def square(t):
-            nc.scalar.activation(out=junk[:], in_=rows[t], func=ACT.Square, accum_out=x2[:, t : t + 1])
-            if t % GR == GR - 1:
-                g = t // GR
-                casts_g(t + GR)
-                nc.gpsimd.tensor_scalar(
-                    out=nb[:, g * GR : (g + 1) * GR], in0=x2[:, g * GR : (g + 1) * GR],
-                    scalar1=-5.0, scalar2=0.0, op0=ALU.mult, op1=ALU.add,
-                )
+            nc.scalar.activation(
+                out=junk[:], in_=rows[t], func=ACT.Square, scale=ROOT_HALF, accum_out=x2h[:, t : t + 1],
+            )
 
         def store(r0, r1):
             c = r0 // CH
@@ -173,60 +180,77 @@ def tile_dicgaussianrbf_t_kernel(tc, data, centers, out):
             nc.sync.dma_start(out=out_v[:, c * CH * W + a : c * CH * W + b], in_=o_tiles[c][:, a:b])
 
         def expo(t):
-            nc.scalar.activation(
-                out=o_row(t)[:, 1 + D : W], in_=tmp_of[t][:], func=ACT.Exp,
-                bias=nb[:, t : t + 1], scale=10.0,
-            )
+            nc.scalar.activation(out=o_row(t)[:, 1 + D : W], in_=tmp_of[t][:], func=ACT.Exp, scale=10.0)
             if t + 1 in STORE_CUTS:
                 store(st["cut"], t + 1)
                 st["cut"] = t + 1
 
         def passes(t_done):
-            for r in range(st["m"], min(t_done + GR, T - 1) + 1):
-                if r // GR in quant:
+            for r in range(st["m"], min(t_done + XC_BUFS, T - 1) + 1):
+                if r < st["ready"]:
                     mx(r)
                     st["m"] = r + 1
+
+        for c in range(T // CH):
+            nc.gpsimd.memset(o_views[c][:, :, 0:1], 1.0)
+        for t in range(T):
+            nc.gpsimd.tensor_scalar(
+                out=o_row(t)[:, 1 : 1 + D], in0=rows[t], scalar1=1.0, scalar2=0.0, op0=ALU.mult, op1=ALU.add,
+            )
 
         transposes("c", [cen[:, j, :] for j in range(4)])
         t_data(0)
         for j in range(4):
-            nc.scalar.activation(out=junk[:], in_=cen[:, j, :], func=ACT.Square, accum_out=c2col[:, j : j + 1])
+            nc.scalar.activation(
+                out=junk[:], in_=cen[:, j, :], func=ACT.Square, scale=ROOT_HALF, accum_out=c2col[:, j : j + 1],
+            )
         copy_out("c", 0)
         copy_out("c", 1)
-        copy_out(0, 0)
-        copy_out(0, 1)
-        t_data(1)
+        copy_out(0, 0, on_scalar=True)
         quantise("c")
-        nc.vector.tensor_copy(out=rep[:], in_=c2col[:].unsqueeze(2).to_broadcast([P, 4, P]))
-        c2ps = psum.tile([P, K], F32, tag="xc", name="c2ps")
+        quantise(0, 0, 256)
+        c2ps = psum.tile([P, K], F32, tag="gm", name="c2ps", bufs=1)
         for j in range(4):
-            nc.tensor.transpose(c2ps[:, j * P : (j + 1) * P], rep[:, j, :], ident[:])
-        quantise(0)
-        for t in range(min(2, VROWS)):
-            cast_v(t)
-        nc.vector.tensor_scalar(out=c2h[:], in0=c2ps[:], scalar1=0.5, scalar2=None, op0=ALU.mult)
+            nc.tensor.transpose(
+                c2ps[:, j * P : (j + 1) * P], c2col[:, j : j + 1].to_broadcast([P, P]), ident[:]
+            )
+        nc.vector.tensor_copy(out=c2h[:], in_=c2ps[:])
+        square(0)
+        square(1)
         passes(-1)
-        t_data(2)
-        for t in range(LEAD):
-            square(t)
+        copy_out(0, 1, on_scalar=True)
+        square(2)
+        t_data(1)
 
-        aux = []
-        for g in range(1, NG):
-            aux.extend([("c", g, 0), ("c", g, 1), ("q", g, 0)])
+        squares = [t for t in range(3, T) if t // GR not in GRAM_GROUPS]
 
         for t in range(T):
-            sub_c2(t)
-            if t + 2 < VROWS:
-                cast_v(t + 2)
+            sub(t)
             expo(t)
-            if t + LEAD < T:
-                square(t + LEAD)
-            if t < len(aux):
-                kind, g, b = aux[t]
-                if kind == "c":
-                    copy_out(g, b)
-                    if b == 1 and g + 2 < NG:
-                        t_data(g + 2)
-                else:
+            if t == 0:
+                quantise(0, 256, 512)
+            g = t // GR + 1
+            ph = t % GR
+            if g < NG:
+                if ph == 0:
+                    copy_out(g, 0)
+                    if g in SCALAR_COPIES:
+                        copy_out(g, 1, on_scalar=True)
+                elif ph == 1:
+                    if g not in SCALAR_COPIES:
+                        copy_out(g, 1)
+                    if g in GRAM_GROUPS:
+                        gram(g)
+                    if g + 1 < NG:
+                        t_data(g + 1)
+                elif ph == 2:
                     quantise(g)
+                elif g in GRAM_GROUPS:
+                    diag(g, 0)
+                    diag(g, 1)
+            if ph == 0 and t // GR in GRAM_GROUPS:
+                diag(t // GR, 2)
+                diag(t // GR, 3)
+            if squares and (squares[0] - t <= 8) and (t < GR or t % 2 == 1 or squares[0] - t <= 4):
+                square(squares.pop(0))
             passes(t)

@@ -127,16 +127,16 @@ def tile_dicgaussianrbf_t_kernel(tc, data, centers, out):
             if key != "c":
                 st["ready"] = key * GR + hi // P
 
-        def gram(g):
-            gm = psum.tile([P, GR, P], F32, tag="gm", name="gm", bufs=1)
+        def gram(g, r):
+            if r == 0:
+                gm = psum.tile([P, GR, P], F32, tag="gm", name="gm", bufs=1)
+                grams[g] = gm
             v = grps[g][:].rearrange("p (r n j) -> p r j n", r=GR, j=4)
-            for r in range(GR):
-                for j in range(4):
-                    nc.tensor.matmul(
-                        out=gm[:, r, :], lhsT=v[:, r, j, :], rhs=v[:, r, j, :],
-                        start=(j == 0), stop=(j == 3),
-                    )
-            grams[g] = gm
+            for j in range(4):
+                nc.tensor.matmul(
+                    out=grams[g][:, r, :], lhsT=v[:, r, j, :], rhs=v[:, r, j, :],
+                    start=(j == 0), stop=(j == 3),
+                )
 
         def diag(g, r):
             t = g * GR + r
@@ -239,18 +239,14 @@ def tile_dicgaussianrbf_t_kernel(tc, data, centers, out):
                 elif ph == 1:
                     if g not in SCALAR_COPIES:
                         copy_out(g, 1)
-                    if g in GRAM_GROUPS:
-                        gram(g)
                     if g + 1 < NG:
                         t_data(g + 1)
                 elif ph == 2:
                     quantise(g)
-                elif g in GRAM_GROUPS:
-                    diag(g, 0)
-                    diag(g, 1)
-            if ph == 0 and t // GR in GRAM_GROUPS:
-                diag(t // GR, 2)
-                diag(t // GR, 3)
             if squares and (squares[0] - t <= 8) and (t < GR or t % 2 == 1 or squares[0] - t <= 4):
                 square(squares.pop(0))
             passes(t)
+            if t + 2 < T and (t + 2) // GR in GRAM_GROUPS:
+                diag((t + 2) // GR, (t + 2) % GR)
+            if t + 3 < T and (t + 3) // GR in GRAM_GROUPS:
+                gram((t + 3) // GR, (t + 3) % GR)

@@ -191,12 +191,13 @@ def tile_dicgaussianrbf_t_kernel(tc, data, centers, out):
                     mx(r)
                     st["m"] = r + 1
 
-        for c in range(T // CH):
-            nc.gpsimd.memset(o_views[c][:, :, 0:1], 1.0)
-        for t in range(T):
-            nc.gpsimd.tensor_scalar(
-                out=o_row(t)[:, 1 : 1 + D], in0=rows[t], scalar1=1.0, scalar2=0.0, op0=ALU.mult, op1=ALU.add,
-            )
+        def casts(t0, t1):
+            nc.vector.memset(o_views[t0 // CH][:, t0 % CH : t0 % CH + t1 - t0, 0:2], 1.0)
+            for t in range(t0, t1):
+                nc.gpsimd.tensor_scalar(
+                    out=o_row(t)[:, 1 : 1 + D], in0=rows[t], scalar1=1.0, scalar2=0.0,
+                    op0=ALU.mult, op1=ALU.add,
+                )
 
         transposes("c", [cen[:, j, :] for j in range(4)])
         t_data(0)
@@ -209,6 +210,7 @@ def tile_dicgaussianrbf_t_kernel(tc, data, centers, out):
         copy_out(0, 0, on_scalar=True)
         quantise("c")
         quantise(0, 0, 256)
+        casts(0, 2)
         c2ps = psum.tile([P, K], F32, tag="gm", name="c2ps", bufs=1)
         for j in range(4):
             nc.tensor.transpose(
@@ -229,6 +231,7 @@ def tile_dicgaussianrbf_t_kernel(tc, data, centers, out):
             expo(t)
             if t == 0:
                 quantise(0, 256, 512)
+                casts(2, 4)
             g = t // GR + 1
             ph = t % GR
             if g < NG:
@@ -243,6 +246,7 @@ def tile_dicgaussianrbf_t_kernel(tc, data, centers, out):
                         t_data(g + 1)
                 elif ph == 2:
                     quantise(g)
+                    casts(g * GR, (g + 1) * GR)
             if squares and (squares[0] - t <= 8) and (t < GR or t % 2 == 1 or squares[0] - t <= 4):
                 square(squares.pop(0))
             passes(t)

@@ -21,13 +21,13 @@ W = 1 + D + K
 T = 4096 // P
 GR = 4
 NG = T // GR
-CH = 8
 LOADS = (4, 4, 8, 8, 8)
 ROOT_HALF = math.sqrt(0.5)
 GRAM_GROUPS = (2, 4, 6)
 SCALAR_COPIES = (1, 2, 3, 4, 5, 6, 7)
 XC_BUFS = 3
-STORE_CUTS = (2, 4, 6, 8, 12, 16, 20, 24, 28, 30, 32)
+SR = 2
+SE = SR * 1024
 
 
 def tile_dicgaussianrbf_t_kernel(tc, data, centers, out):
@@ -60,15 +60,11 @@ def tile_dicgaussianrbf_t_kernel(tc, data, centers, out):
                 rows.append(dtile[:, r, :])
             t0 += n
 
-        o_tiles = []
-        o_views = []
-        for c in range(T // CH):
-            ot = keep.tile([P, CH * W], F32, name="o%d" % c)
-            o_tiles.append(ot)
-            o_views.append(ot[:].rearrange("p (t c) -> p t c", c=W))
+        ot = keep.tile([P, T * W], F32, name="ot", align_bytes=256)
+        o_view = ot[:].rearrange("p (t c) -> p t c", c=W)
 
         def o_row(t):
-            return o_views[t // CH][:, t % CH, :]
+            return o_view[:, t, :]
 
         x2h = keep.tile([P, T], F32, name="x2h")
         c2col = keep.tile([P, 4], F32, name="c2col")
@@ -84,7 +80,7 @@ def tile_dicgaussianrbf_t_kernel(tc, data, centers, out):
         xcs = {}
         grams = {}
         tmp_of = {}
-        st = {"cut": 0, "m": 0, "ready": 0}
+        st = {"m": 0, "ready": 0}
 
         def transposes(key, srcs):
             pair = []
@@ -173,17 +169,15 @@ def tile_dicgaussianrbf_t_kernel(tc, data, centers, out):
                 out=junk[:], in_=rows[t], func=ACT.Square, scale=ROOT_HALF, accum_out=x2h[:, t : t + 1],
             )
 
-        def store(r0, r1):
-            c = r0 // CH
-            a = ((r0 % CH) * W) // 8 * 8
-            b = CH * W if r1 % CH == 0 else ((r1 % CH) * W) // 8 * 8
-            nc.sync.dma_start(out=out_v[:, c * CH * W + a : c * CH * W + b], in_=o_tiles[c][:, a:b])
+        def store(i):
+            a = i * SE
+            b = T * W if (i + 1) * SR == T else a + SE
+            nc.sync.dma_start(out=out_v[:, a:b], in_=ot[:, a:b])
 
         def expo(t):
             nc.scalar.activation(out=o_row(t)[:, 1 + D : W], in_=tmp_of[t][:], func=ACT.Exp, scale=10.0)
-            if t + 1 in STORE_CUTS:
-                store(st["cut"], t + 1)
-                st["cut"] = t + 1
+            if t % SR == SR - 1:
+                store(t // SR)
 
         def passes(t_done):
             for r in range(st["m"], min(t_done + XC_BUFS, T - 1) + 1):
@@ -192,7 +186,7 @@ def tile_dicgaussianrbf_t_kernel(tc, data, centers, out):
                     st["m"] = r + 1
 
         def casts(t0, t1):
-            nc.vector.memset(o_views[t0 // CH][:, t0 % CH : t0 % CH + t1 - t0, 0:2], 1.0)
+            nc.vector.memset(o_view[:, t0:t1, 0:2], 1.0)
             for t in range(t0, t1):
                 nc.gpsimd.tensor_scalar(
                     out=o_row(t)[:, 1 : 1 + D], in0=rows[t], scalar1=1.0, scalar2=0.0,

@@ -26,7 +26,7 @@ ROOT_HALF = math.sqrt(0.5)
 GRAM_GROUPS = (2, 4, 6)
 SCALAR_COPIES = (1, 2, 3, 4, 5, 6, 7)
 XC_BUFS = 3
-SR = 2
+SR = 1
 SE = SR * 1024
 
 

@@ -23,9 +23,9 @@ GR = 4
 NG = T // GR
 LOADS = (4, 4, 8, 8, 8)
 ROOT_HALF = math.sqrt(0.5)
-GRAM_GROUPS = (2, 4, 6)
-SCALAR_COPIES = (1, 2, 3, 4, 5, 6, 7)
-XC_BUFS = 3
+BN_GROUPS = (2, 4, 6)
+XC_BUFS = 4
+SQ_LEAD = 4
 SR = 1
 SE = SR * 1024
 
@@ -67,18 +67,19 @@ def tile_dicgaussianrbf_t_kernel(tc, data, centers, out):
             return o_view[:, t, :]
 
         x2h = keep.tile([P, T], F32, name="x2h")
+        x2v = keep.tile([P, NG], F32, name="x2v")
         c2col = keep.tile([P, 4], F32, name="c2col")
         junk = keep.tile([P, D], BF16, name="junk")
-        junk_g = keep.tile([P, P], F32, name="junk_g")
         c2h = keep.tile([P, K], F32, name="c2h")
         c_codes = keep.tile([P, K], U32, name="c_codes", align_bytes=64)
         c_scl = keep.tile([P, K], U8, name="c_scl", align_bytes=64)
 
+        bn_rows = [g * GR + GR - 1 for g in BN_GROUPS]
         banks = {}
         grps = {}
         quant = {}
         xcs = {}
-        grams = {}
+        stat_of = {}
         tmp_of = {}
         st = {"m": 0, "ready": 0}
 
@@ -123,22 +124,21 @@ def tile_dicgaussianrbf_t_kernel(tc, data, centers, out):
             if key != "c":
                 st["ready"] = key * GR + hi // P
 
-        def gram(g, r):
-            if r == 0:
-                gm = psum.tile([P, GR, P], F32, tag="gm", name="gm", bufs=1)
-                grams[g] = gm
-            v = grps[g][:].rearrange("p (r n j) -> p r j n", r=GR, j=4)
-            for j in range(4):
-                nc.tensor.matmul(
-                    out=grams[g][:, r, :], lhsT=v[:, r, j, :], rhs=v[:, r, j, :],
-                    start=(j == 0), stop=(j == 3),
-                )
+        def stats(t):
+            st6 = tmps.tile([P, 6], F32, tag="st6", name="st6")
+            nc.vector.bn_stats(out=st6[:], in_=rows[t])
+            stat_of[t] = st6
 
-        def diag(g, r):
-            t = g * GR + r
-            nc.vector.scalar_tensor_tensor(
-                out=junk_g[:], in0=grams[g][:, r, :], scalar=0.5, in1=ident[:],
-                op0=ALU.mult, op1=ALU.mult, accum_out=x2h[:, t : t + 1],
+        def from_stats(t):
+            mv = tmps.tile([P, 2], F32, tag="mv", name="mv")
+            nc.vector.bn_aggr(out=mv[:], in_=stat_of[t][:])
+            sq = tmps.tile([P, 1], F32, tag="sq", name="sq")
+            nc.gpsimd.tensor_scalar(
+                out=sq[:], in0=mv[:, 0:1], scalar1=mv[:, 0:1], scalar2=D / 2.0, op0=ALU.mult, op1=ALU.mult,
+            )
+            nc.gpsimd.tensor_scalar(
+                out=x2v[:, t // GR : t // GR + 1], in0=mv[:, 1:2], scalar1=D / 2.0, scalar2=sq[:],
+                op0=ALU.mult, op1=ALU.add,
             )
 
         def mx(t):
@@ -158,8 +158,9 @@ def tile_dicgaussianrbf_t_kernel(tc, data, centers, out):
 
         def sub(t):
             tmp = tmps.tile([P, K], F32, tag="tmp", name="tmp")
+            half = x2v[:, t // GR : t // GR + 1] if t in bn_rows else x2h[:, t : t + 1]
             nc.vector.scalar_tensor_tensor(
-                out=tmp[:], in0=xcs[t][:], scalar=x2h[:, t : t + 1], in1=c2h[:],
+                out=tmp[:], in0=xcs[t][:], scalar=half, in1=c2h[:],
                 op0=ALU.subtract, op1=ALU.subtract,
             )
             tmp_of[t] = tmp
@@ -205,7 +206,7 @@ def tile_dicgaussianrbf_t_kernel(tc, data, centers, out):
         quantise("c")
         quantise(0, 0, 256)
         casts(0, 2)
-        c2ps = psum.tile([P, K], F32, tag="gm", name="c2ps", bufs=1)
+        c2ps = psum.tile([P, K], F32, tag="xc", name="c2ps", bufs=XC_BUFS)
         for j in range(4):
             nc.tensor.transpose(
                 c2ps[:, j * P : (j + 1) * P], c2col[:, j : j + 1].to_broadcast([P, P]), ident[:]
@@ -218,7 +219,7 @@ def tile_dicgaussianrbf_t_kernel(tc, data, centers, out):
         square(2)
         t_data(1)
 
-        squares = [t for t in range(3, T) if t // GR not in GRAM_GROUPS]
+        squares = [t for t in range(3, T) if t not in bn_rows]
 
         for t in range(T):
             sub(t)
@@ -231,20 +232,17 @@ def tile_dicgaussianrbf_t_kernel(tc, data, centers, out):
             if g < NG:
                 if ph == 0:
                     copy_out(g, 0)
-                    if g in SCALAR_COPIES:
-                        copy_out(g, 1, on_scalar=True)
                 elif ph == 1:
-                    if g not in SCALAR_COPIES:
-                        copy_out(g, 1)
+                    copy_out(g, 1)
                     if g + 1 < NG:
                         t_data(g + 1)
                 elif ph == 2:
                     quantise(g)
                     casts(g * GR, (g + 1) * GR)
-            if squares and (squares[0] - t <= 8) and (t < GR or t % 2 == 1 or squares[0] - t <= 4):
+                elif g in BN_GROUPS:
+                    stats(g * GR + GR - 1)
+            if ph == 0 and t // GR in BN_GROUPS:
+                from_stats(t + GR - 1)
+            if squares and squares[0] - t <= SQ_LEAD:
                 square(squares.pop(0))
             passes(t)
-            if t + 2 < T and (t + 2) // GR in GRAM_GROUPS:
-                diag((t + 2) // GR, (t + 2) % GR)
-            if t + 3 < T and (t + 3) // GR in GRAM_GROUPS:
-                gram((t + 3) // GR, (t + 3) % GR)

@@ -23,11 +23,10 @@ GR = 4
 NG = T // GR
 LOADS = (4, 4, 8, 8, 8)
 ROOT_HALF = math.sqrt(0.5)
-BN_GROUPS = (2, 4, 6)
-XC_BUFS = 4
+GRAM_ROWS = 1
+XC_BUFS = 3
 SQ_LEAD = 4
-SR = 1
-SE = SR * 1024
+SE = 1024
 
 
 def tile_dicgaussianrbf_t_kernel(tc, data, centers, out):
@@ -50,7 +49,7 @@ def tile_dicgaussianrbf_t_kernel(tc, data, centers, out):
         nc.scalar.activation(out=warm2[:], in_=warm[:], func=ACT.Exp)
 
         cen = keep.tile([P, 4, D], BF16, name="cen")
-        nc.sync.dma_start(out=cen[:], in_=centers.rearrange("(j p) d -> p j d", p=P))
+        nc.sync.dma_start(out=cen[:], in_=centers.rearrange("(p j) d -> p j d", j=4))
         rows = []
         t0 = 0
         for li, n in enumerate(LOADS):
@@ -67,19 +66,18 @@ def tile_dicgaussianrbf_t_kernel(tc, data, centers, out):
             return o_view[:, t, :]
 
         x2h = keep.tile([P, T], F32, name="x2h")
-        x2v = keep.tile([P, NG], F32, name="x2v")
         c2col = keep.tile([P, 4], F32, name="c2col")
         junk = keep.tile([P, D], BF16, name="junk")
+        junk_g = keep.tile([P, P], F32, name="junk_g")
         c2h = keep.tile([P, K], F32, name="c2h")
         c_codes = keep.tile([P, K], U32, name="c_codes", align_bytes=64)
         c_scl = keep.tile([P, K], U8, name="c_scl", align_bytes=64)
 
-        bn_rows = [g * GR + GR - 1 for g in BN_GROUPS]
         banks = {}
         grps = {}
         quant = {}
         xcs = {}
-        stat_of = {}
+        grams = {}
         tmp_of = {}
         st = {"m": 0, "ready": 0}
 
@@ -103,8 +101,12 @@ def tile_dicgaussianrbf_t_kernel(tc, data, centers, out):
                 grp = work.tile([P, 4 * 512], BF16, tag="grp", name="grp", align_bytes=64)
                 grps[key] = grp
             g32 = grps[key][:].bitcast(F32)
-            dst = g32[:, 512 * b : 512 * (b + 1)].rearrange("q (a n u) -> q a n u", a=2, u=2)
-            src = banks[key][b][:].rearrange("q (a u n) -> q a n u", a=2, u=2)
+            if key == "c":
+                dst = g32.rearrange("q (n b a u) -> q b n a u", b=2, a=2, u=2)[:, b]
+                src = banks[key][b][:].rearrange("q (a u n) -> q n a u", a=2, u=2)
+            else:
+                dst = g32[:, 512 * b : 512 * (b + 1)].rearrange("q (a n u) -> q a n u", a=2, u=2)
+                src = banks[key][b][:].rearrange("q (a u n) -> q a n u", a=2, u=2)
             if on_scalar:
                 nc.scalar.copy(out=dst, in_=src)
             else:
@@ -124,21 +126,22 @@ def tile_dicgaussianrbf_t_kernel(tc, data, centers, out):
             if key != "c":
                 st["ready"] = key * GR + hi // P
 
-        def stats(t):
-            st6 = tmps.tile([P, 6], F32, tag="st6", name="st6")
-            nc.vector.bn_stats(out=st6[:], in_=rows[t])
-            stat_of[t] = st6
+        def gram(g):
+            gm = psum.tile([P, GRAM_ROWS, P], F32, tag="gm", name="gm", bufs=1)
+            v = grps[g][:].rearrange("p (r n j) -> p r j n", r=GR, j=4)
+            for i in range(GRAM_ROWS):
+                r = GR - GRAM_ROWS + i
+                for j in range(4):
+                    nc.tensor.matmul(
+                        out=gm[:, i, :], lhsT=v[:, r, j, :], rhs=v[:, r, j, :], start=(j == 0), stop=(j == 3),
+                    )
+            grams[g] = gm
 
-        def from_stats(t):
-            mv = tmps.tile([P, 2], F32, tag="mv", name="mv")
-            nc.vector.bn_aggr(out=mv[:], in_=stat_of[t][:])
-            sq = tmps.tile([P, 1], F32, tag="sq", name="sq")
-            nc.gpsimd.tensor_scalar(
-                out=sq[:], in0=mv[:, 0:1], scalar1=mv[:, 0:1], scalar2=D / 2.0, op0=ALU.mult, op1=ALU.mult,
-            )
-            nc.gpsimd.tensor_scalar(
-                out=x2v[:, t // GR : t // GR + 1], in0=mv[:, 1:2], scalar1=D / 2.0, scalar2=sq[:],
-                op0=ALU.mult, op1=ALU.add,
+        def diag(g, i):
+            t = (g + 1) * GR - GRAM_ROWS + i
+            nc.vector.scalar_tensor_tensor(
+                out=junk_g[:], in0=grams[g][:, i, :], scalar=0.5, in1=ident[:],
+                op0=ALU.mult, op1=ALU.mult, accum_out=x2h[:, t : t + 1],
             )
 
         def mx(t):
@@ -158,9 +161,8 @@ def tile_dicgaussianrbf_t_kernel(tc, data, centers, out):
 
         def sub(t):
             tmp = tmps.tile([P, K], F32, tag="tmp", name="tmp")
-            half = x2v[:, t // GR : t // GR + 1] if t in bn_rows else x2h[:, t : t + 1]
             nc.vector.scalar_tensor_tensor(
-                out=tmp[:], in0=xcs[t][:], scalar=half, in1=c2h[:],
+                out=tmp[:], in0=xcs[t][:], scalar=x2h[:, t : t + 1], in1=c2h[:],
                 op0=ALU.subtract, op1=ALU.subtract,
             )
             tmp_of[t] = tmp
@@ -172,13 +174,12 @@ def tile_dicgaussianrbf_t_kernel(tc, data, centers, out):
 
         def store(i):
             a = i * SE
-            b = T * W if (i + 1) * SR == T else a + SE
+            b = T * W if i + 1 == T else a + SE
             nc.sync.dma_start(out=out_v[:, a:b], in_=ot[:, a:b])
 
         def expo(t):
             nc.scalar.activation(out=o_row(t)[:, 1 + D : W], in_=tmp_of[t][:], func=ACT.Exp, scale=10.0)
-            if t % SR == SR - 1:
-                store(t // SR)
+            store(t)
 
         def passes(t_done):
             for r in range(st["m"], min(t_done + XC_BUFS, T - 1) + 1):
@@ -206,12 +207,14 @@ def tile_dicgaussianrbf_t_kernel(tc, data, centers, out):
         quantise("c")
         quantise(0, 0, 256)
         casts(0, 2)
-        c2ps = psum.tile([P, K], F32, tag="xc", name="c2ps", bufs=XC_BUFS)
+        c2ps = psum.tile([P, K], F32, tag="gm", name="c2ps", bufs=1)
         for j in range(4):
             nc.tensor.transpose(
                 c2ps[:, j * P : (j + 1) * P], c2col[:, j : j + 1].to_broadcast([P, P]), ident[:]
             )
-        nc.vector.tensor_copy(out=c2h[:], in_=c2ps[:])
+        nc.vector.tensor_copy(
+            out=c2h[:].rearrange("p (n j) -> p n j", j=4), in_=c2ps[:].rearrange("p (j n) -> p n j", j=4)
+        )
         square(0)
         square(1)
         passes(-1)
@@ -219,7 +222,7 @@ def tile_dicgaussianrbf_t_kernel(tc, data, centers, out):
         square(2)
         t_data(1)
 
-        squares = [t for t in range(3, T) if t not in bn_rows]
+        squares = [t for t in range(3, T) if t < GR or t % GR < GR - GRAM_ROWS]
 
         for t in range(T):
             sub(t)
@@ -239,10 +242,11 @@ def tile_dicgaussianrbf_t_kernel(tc, data, centers, out):
                 elif ph == 2:
                     quantise(g)
                     casts(g * GR, (g + 1) * GR)
-                elif g in BN_GROUPS:
-                    stats(g * GR + GR - 1)
-            if ph == 0 and t // GR in BN_GROUPS:
-                from_stats(t + GR - 1)
+                else:
+                    for i in range(GRAM_ROWS):
+                        diag(g, i)
             if squares and squares[0] - t <= SQ_LEAD:
                 square(squares.pop(0))
             passes(t)
+            if ph == 1 and g < NG:
+                gram(g)

@@ -21,12 +21,12 @@ W = 1 + D + K
 T = 4096 // P
 GR = 4
 NG = T // GR
-LOADS = (4, 4, 8, 8, 8)
+LOADS = (4, 4, 8, 16)
 ROOT_HALF = math.sqrt(0.5)
 GRAM_ROWS = 1
 XC_BUFS = 3
 SQ_LEAD = 4
-SE = 1024
+STORE_CUTS = tuple(range(1, 17)) + tuple(range(18, T + 1, 2))
 
 
 def tile_dicgaussianrbf_t_kernel(tc, data, centers, out):
@@ -79,7 +79,7 @@ def tile_dicgaussianrbf_t_kernel(tc, data, centers, out):
         xcs = {}
         grams = {}
         tmp_of = {}
-        st = {"m": 0, "ready": 0}
+        st = {"cut": 0, "m": 0, "ready": 0}
 
         def transposes(key, srcs):
             pair = []
@@ -172,14 +172,16 @@ def tile_dicgaussianrbf_t_kernel(tc, data, centers, out):
                 out=junk[:], in_=rows[t], func=ACT.Square, scale=ROOT_HALF, accum_out=x2h[:, t : t + 1],
             )
 
-        def store(i):
-            a = i * SE
-            b = T * W if i + 1 == T else a + SE
+        def store(r0, r1):
+            a = r0 * 1024
+            b = T * W if r1 == T else r1 * 1024
             nc.sync.dma_start(out=out_v[:, a:b], in_=ot[:, a:b])
 
         def expo(t):
             nc.scalar.activation(out=o_row(t)[:, 1 + D : W], in_=tmp_of[t][:], func=ACT.Exp, scale=10.0)
-            store(t)
+            if t + 1 in STORE_CUTS:
+                store(st["cut"], t + 1)
+                st["cut"] = t + 1
 
         def passes(t_done):
             for r in range(st["m"], min(t_done + XC_BUFS, T - 1) + 1):

import math
from contextlib import ExitStack

import concourse.masks as masks
import concourse.mybir as mybir

FLOPS = 2 * 4096 * 512 * 512

F32 = mybir.dt.float32
BF16 = mybir.dt.bfloat16
U32 = mybir.dt.uint32
U8 = mybir.dt.uint8
FP8X4 = mybir.dt.float8_e4m3fn_x4
ACT = mybir.ActivationFunctionType
ALU = mybir.AluOpType

P = 128
D = 512
K = 512
W = 1 + D + K
T = 4096 // P
GR = 4
NG = T // GR
LOADS = (4, 4, 8, 16)
ROOT_HALF = math.sqrt(0.5)
GRAM_ROWS = 1
XC_BUFS = 3
SQ_LEAD = 4
STORE_CUTS = tuple(range(1, 17)) + tuple(range(18, T + 1, 2))


def tile_dicgaussianrbf_t_kernel(tc, data, centers, out):
    nc = tc.nc
    with ExitStack() as ctx:
        keep = ctx.enter_context(tc.tile_pool(name="keep", bufs=1))
        work = ctx.enter_context(tc.tile_pool(name="work", bufs=3))
        tmps = ctx.enter_context(tc.tile_pool(name="tmps", bufs=6))
        psum = ctx.enter_context(tc.psum_pool(name="psum", bufs=4))
        ctx.enter_context(tc.manual_schedule())

        data_v = data.rearrange("(p t) d -> p t d", t=T)
        out_v = out.rearrange("(p t) c -> p (t c)", t=T)

        ident = keep.tile([P, P], F32, name="ident")
        masks.make_identity(nc, ident[:])
        warm = keep.tile([P, 1], F32, name="warm")
        warm2 = keep.tile([P, 1], F32, name="warm2")
        nc.vector.memset(warm[:], 0.0)
        nc.scalar.activation(out=warm2[:], in_=warm[:], func=ACT.Exp)

        cen = keep.tile([P, 4, D], BF16, name="cen")
        nc.sync.dma_start(out=cen[:], in_=centers.rearrange("(p j) d -> p j d", j=4))
        rows = []
        t0 = 0
        for li, n in enumerate(LOADS):
            dtile = keep.tile([P, n, D], BF16, name="d%d" % li)
            nc.sync.dma_start(out=dtile[:], in_=data_v[:, t0 : t0 + n, :])
            for r in range(n):
                rows.append(dtile[:, r, :])
            t0 += n

        ot = keep.tile([P, T * W], F32, name="ot", align_bytes=256)
        o_view = ot[:].rearrange("p (t c) -> p t c", c=W)

        def o_row(t):
            return o_view[:, t, :]

        x2h = keep.tile([P, T], F32, name="x2h")
        c2col = keep.tile([P, 4], F32, name="c2col")
        junk = keep.tile([P, D], BF16, name="junk")
        junk_g = keep.tile([P, P], F32, name="junk_g")
        c2h = keep.tile([P, K], F32, name="c2h")
        c_codes = keep.tile([P, K], U32, name="c_codes", align_bytes=64)
        c_scl = keep.tile([P, K], U8, name="c_scl", align_bytes=64)

        banks = {}
        grps = {}
        quant = {}
        xcs = {}
        grams = {}
        tmp_of = {}
        st = {"cut": 0, "m": 0, "ready": 0}

        def transposes(key, srcs):
            pair = []
            for b in range(2):
                tp = psum.tile([P, 512], F32, tag="tp", name="tp")
                for a in range(2):
                    src = srcs[2 * b + a].bitcast(F32)
                    for u in range(2):
                        s = (2 * a + u) * P
                        nc.tensor.transpose(tp[:, s : s + P], src[:, u * P : (u + 1) * P], ident[:])
                pair.append(tp)
            banks[key] = pair

        def t_data(g):
            transposes(g, rows[g * GR : (g + 1) * GR])

        def copy_out(key, b, on_scalar=False):
            if key not in grps:
                grp = work.tile([P, 4 * 512], BF16, tag="grp", name="grp", align_bytes=64)
                grps[key] = grp
            g32 = grps[key][:].bitcast(F32)
            if key == "c":
                dst = g32.rearrange("q (n b a u) -> q b n a u", b=2, a=2, u=2)[:, b]
                src = banks[key][b][:].rearrange("q (a u n) -> q n a u", a=2, u=2)
            else:
                dst = g32[:, 512 * b : 512 * (b + 1)].rearrange("q (a n u) -> q a n u", a=2, u=2)
                src = banks[key][b][:].rearrange("q (a u n) -> q a n u", a=2, u=2)
            if on_scalar:
                nc.scalar.copy(out=dst, in_=src)
            else:
                nc.vector.tensor_copy(out=dst, in_=src)

        def quantise(key, lo=0, hi=512):
            if key == "c":
                quant[key] = (c_codes, c_scl)
            elif key not in quant:
                codes = work.tile([P, 512], U32, tag="codes", name="codes", align_bytes=64)
                scl = work.tile([P, 512], U8, tag="scl", name="scl", align_bytes=64)
                quant[key] = (codes, scl)
            codes, scl = quant[key]
            nc.vector.quantize_mx(
                out=codes[:, lo:hi].bitcast(FP8X4), scales=scl[:, lo:hi], in_=grps[key][:, 4 * lo : 4 * hi]
            )
            if key != "c":
                st["ready"] = key * GR + hi // P

        def gram(g):
            gm = psum.tile([P, GRAM_ROWS, P], F32, tag="gm", name="gm", bufs=1)
            v = grps[g][:].rearrange("p (r n j) -> p r j n", r=GR, j=4)
            for i in range(GRAM_ROWS):
                r = GR - GRAM_ROWS + i
                for j in range(4):
                    nc.tensor.matmul(
                        out=gm[:, i, :], lhsT=v[:, r, j, :], rhs=v[:, r, j, :], start=(j == 0), stop=(j == 3),
                    )
            grams[g] = gm

        def diag(g, i):
            t = (g + 1) * GR - GRAM_ROWS + i
            nc.vector.scalar_tensor_tensor(
                out=junk_g[:], in0=grams[g][:, i, :], scalar=0.5, in1=ident[:],
                op0=ALU.mult, op1=ALU.mult, accum_out=x2h[:, t : t + 1],
            )

        def mx(t):
            codes, scl = quant[t // GR]
            a = t % GR
            xc = psum.tile([P, K], F32, tag="xc", name="xc", bufs=XC_BUFS)
            nc.tensor.matmul_mx(
                out=xc[:],
                lhsT=codes[:, a * P : (a + 1) * P].bitcast(FP8X4),
                lhsT_scale=scl[:, a * P : (a + 1) * P],
                rhs=c_codes[:].bitcast(FP8X4),
                rhs_scale=c_scl[:],
                start=True,
                stop=True,
            )
            xcs[t] = xc

        def sub(t):
            tmp = tmps.tile([P, K], F32, tag="tmp", name="tmp")
            nc.vector.scalar_tensor_tensor(
                out=tmp[:], in0=xcs[t][:], scalar=x2h[:, t : t + 1], in1=c2h[:],
                op0=ALU.subtract, op1=ALU.subtract,
            )
            tmp_of[t] = tmp

        def square(t):
            nc.scalar.activation(
                out=junk[:], in_=rows[t], func=ACT.Square, scale=ROOT_HALF, accum_out=x2h[:, t : t + 1],
            )

        def store(r0, r1):
            a = r0 * 1024
            b = T * W if r1 == T else r1 * 1024
            nc.sync.dma_start(out=out_v[:, a:b], in_=ot[:, a:b])

        def expo(t):
            nc.scalar.activation(out=o_row(t)[:, 1 + D : W], in_=tmp_of[t][:], func=ACT.Exp, scale=10.0)
            if t + 1 in STORE_CUTS:
                store(st["cut"], t + 1)
                st["cut"] = t + 1

        def passes(t_done):
            for r in range(st["m"], min(t_done + XC_BUFS, T - 1) + 1):
                if r < st["ready"]:
                    mx(r)
                    st["m"] = r + 1

        def casts(t0, t1):
            nc.vector.memset(o_view[:, t0:t1, 0:2], 1.0)
            for t in range(t0, t1):
                nc.gpsimd.tensor_scalar(
                    out=o_row(t)[:, 1 : 1 + D], in0=rows[t], scalar1=1.0, scalar2=0.0,
                    op0=ALU.mult, op1=ALU.add,
                )

        transposes("c", [cen[:, j, :] for j in range(4)])
        t_data(0)
        for j in range(4):
            nc.scalar.activation(
                out=junk[:], in_=cen[:, j, :], func=ACT.Square, scale=ROOT_HALF, accum_out=c2col[:, j : j + 1],
            )
        copy_out("c", 0)
        copy_out("c", 1)
        copy_out(0, 0, on_scalar=True)
        quantise("c")
        quantise(0, 0, 256)
        casts(0, 2)
        c2ps = psum.tile([P, K], F32, tag="gm", name="c2ps", bufs=1)
        for j in range(4):
            nc.tensor.transpose(
                c2ps[:, j * P : (j + 1) * P], c2col[:, j : j + 1].to_broadcast([P, P]), ident[:]
            )
        nc.vector.tensor_copy(
            out=c2h[:].rearrange("p (n j) -> p n j", j=4), in_=c2ps[:].rearrange("p (j n) -> p n j", j=4)
        )
        square(0)
        square(1)
        passes(-1)
        copy_out(0, 1, on_scalar=True)
        square(2)
        t_data(1)

        squares = [t for t in range(3, T) if t < GR or t % GR < GR - GRAM_ROWS]

        for t in range(T):
            sub(t)
            expo(t)
            if t == 0:
                quantise(0, 256, 512)
                casts(2, 4)
            g = t // GR + 1
            ph = t % GR
            if g < NG:
                if ph == 0:
                    copy_out(g, 0)
                elif ph == 1:
                    copy_out(g, 1)
                    if g + 1 < NG:
                        t_data(g + 1)
                elif ph == 2:
                    quantise(g)
                    casts(g * GR, (g + 1) * GR)
                else:
                    for i in range(GRAM_ROWS):
                        diag(g, i)
            if squares and squares[0] - t <= SQ_LEAD:
                square(squares.pop(0))
            passes(t)
            if ph == 1 and g < NG:
                gram(g)
